import numpy as np
import ml_dtypes

BF16 = ml_dtypes.bfloat16


def bf(x):
    return np.asarray(x, np.float32).astype(BF16)


def f32(x):
    return np.asarray(x, np.float32)


def f64(x):
    return np.asarray(x).astype(np.float64)


def striped(idx):
    return np.tile(idx.reshape(-1, 16).T, (8, 1))


T, H, D, DV, S, L, N = 2, 128, 128, 128, 2048, 128, 256
SCALE = 192.0 ** -0.5


def setup_inputs():
    return {"table": bf(np.random.standard_normal((S, D))), "w": bf(2.0 * np.random.standard_normal((D, T * H))), "sink": f32(5.0 + np.random.standard_normal((H, 1))), "offs": striped(np.random.permutation(S)[:N])}


def reference(table, w, sink, offs):
    idx = offs[:16].T.reshape(-1)
    tab = f64(table)
    q = f64(w)
    sk = f64(sink)
    cols = []
    for t in range(T):
        k = tab[idx[t * L:(t + 1) * L]]
        a = SCALE * (q[:, t * H:(t + 1) * H].T @ k.T)
        e = np.exp(a)
        p = e / (e.sum(axis=1, keepdims=True) + np.exp(sk))
        cols.append(k[:, :DV].T @ p.T)
    return np.concatenate(cols, axis=1)

@@ -1,0 +1,126 @@
+import concourse.mybir as mybir
+from concourse.masks import make_identity
+
+BF16, F32, U16 = mybir.dt.bfloat16, mybir.dt.float32, mybir.dt.uint16
+EXP = mybir.ActivationFunctionType.Exp
+MULT = mybir.AluOpType.mult
+FREE_AXIS = mybir.AxisListType.X
+
+P = 128
+TOKENS = 2
+SLOTS = 2048
+BLOCKS = SLOTS // P
+CHUNK = 4
+PIECE = 128
+PIECE_COLS = PIECE // 16
+SCALE = 192.0**-0.5
+
+FLOPS = 2 * (2 * TOKENS * P * PIECE * P)
+
+
+def tile_deepseekv4mlaattention_kernel(tc, table, w, sink, offs, out):
+    nc = tc.nc
+    with (
+        tc.tile_pool(name="held", bufs=1) as held,
+        tc.psum_pool(name="psum", bufs=1) as psum,
+    ):
+        offsets = held.tile([P, TOKENS * PIECE_COLS], U16, name="offsets")
+        nc.sync.dma_start(offsets[:], offs)
+
+        rows = held.tile([P, BLOCKS, P], BF16, name="rows")
+        table_blocks = table.rearrange("(b p) d -> p b d", p=P)
+        for first in range(0, BLOCKS, CHUNK):
+            queue = nc.sync if (first // CHUNK) % 2 == 0 else nc.scalar
+            queue.dma_start(
+                rows[:, first : first + CHUNK, :], table_blocks[:, first : first + CHUNK, :]
+            )
+
+        queries = held.tile([P, TOKENS * P], BF16, name="queries")
+        nc.gpsimd.dma_start(queries[:], w)
+
+        sink_row = held.tile([1, P], F32, name="sink_row")
+        nc.gpsimd.dma_start(sink_row[:], sink.rearrange("h one -> one h"))
+
+        identity = held.tile([P, P], BF16, name="identity")
+        make_identity(nc, identity[:])
+
+        unscale = held.tile([1, 1], F32, name="unscale")
+        nc.vector.memset(unscale[:], 1.0 / SCALE)
+
+        zero = held.tile([P, 1], F32, name="zero")
+        one = held.tile([P, 1], F32, name="one")
+        nc.vector.memset(zero[:], 0.0)
+        nc.scalar.activation(one[:], zero[:], EXP)
+
+        flipped = held.tile([P, SLOTS], BF16, name="flipped")
+        with tc.psum_pool(name="flip_psum", bufs=1) as flip_psum:
+            for first in range(0, BLOCKS, CHUNK):
+                flipped_ps = flip_psum.tile([P, CHUNK * P], BF16, name=f"flipped_ps{first}")
+                for k in range(CHUNK):
+                    nc.tensor.transpose(
+                        flipped_ps[:, k * P : (k + 1) * P], rows[:, first + k, :], identity[:]
+                    )
+                chunk_of_window = flipped[:, first * P : (first + CHUNK) * P]
+                if (first // CHUNK) % 2 == 0:
+                    nc.vector.tensor_copy(chunk_of_window, flipped_ps[:])
+                else:
+                    nc.scalar.copy(chunk_of_window, flipped_ps[:])
+
+        logits = [psum.tile([P, PIECE + 1], F32, name=f"logits{t}") for t in range(TOKENS)]
+        for t in range(TOKENS):
+            nc.tensor.matmul(
+                logits[t][:, PIECE : PIECE + 1], sink_row[:], unscale[:], start=True, stop=True
+            )
+        for t in range(TOKENS):
+            piece = offsets[:, t * PIECE_COLS : (t + 1) * PIECE_COLS]
+            nc.tensor.matmul(
+                logits[t][:, 0:PIECE],
+                queries[:, t * P : (t + 1) * P],
+                flipped[:].indirect(piece),
+                start=True,
+                stop=True,
+            )
+
+        picked_ps = psum.tile([P, TOKENS * PIECE], F32, name="picked_ps")
+        nc.tensor.matmul(
+            picked_ps[:], identity[:], flipped[:].indirect(offsets[:]), start=True, stop=True
+        )
+        picked = held.tile([P, TOKENS * PIECE], BF16, name="picked")
+        nc.vector.tensor_copy(picked[:], picked_ps[:])
+        values_ps = psum.tile([P, TOKENS * P], BF16, name="values_ps")
+        for t in range(TOKENS):
+            nc.tensor.transpose(
+                values_ps[:, t * P : (t + 1) * P], picked[:, t * PIECE : (t + 1) * PIECE], identity[:]
+            )
+        values = held.tile([P, TOKENS * P], BF16, name="values")
+        nc.scalar.copy(values[:], values_ps[:])
+
+        with tc.psum_pool(name="late_psum", bufs=1) as late_psum:
+            for t in range(TOKENS):
+                top = held.tile([P, 1], F32, name=f"top{t}")
+                nc.vector.reduce_max(top[:], logits[t][:], axis=FREE_AXIS)
+                shift = held.tile([P, 1], F32, name=f"shift{t}")
+                nc.vector.tensor_scalar(shift[:], top[:], -SCALE, None, op0=MULT)
+
+                weights = held.tile([P, PIECE + 1], F32, name=f"weights{t}")
+                total = held.tile([P, 1], F32, name=f"total{t}")
+                nc.scalar.activation(
+                    weights[:], logits[t][:], EXP, bias=shift[:], scale=SCALE, accum_out=total[:]
+                )
+                inverse = held.tile([P, 1], F32, name=f"inverse{t}")
+                nc.vector.reciprocal(inverse[:], total[:])
+                probs = held.tile([P, PIECE], BF16, name=f"probs{t}")
+                nc.vector.tensor_scalar(probs[:], weights[:, 0:PIECE], inverse[:], None, op0=MULT)
+
+                probs_t_ps = late_psum.tile([P, P], BF16, name=f"probs_t_ps{t}")
+                nc.tensor.transpose(probs_t_ps[:], probs[:], identity[:])
+                probs_t = held.tile([P, P], BF16, name=f"probs_t{t}")
+                nc.vector.tensor_copy(probs_t[:], probs_t_ps[:])
+
+                mixed_ps = late_psum.tile([P, P], F32, name=f"mixed_ps{t}")
+                nc.tensor.matmul(
+                    mixed_ps[:], values[:, t * P : (t + 1) * P], probs_t[:], start=True, stop=True
+                )
+                mixed = held.tile([P, P], F32, name=f"mixed{t}")
+                nc.vector.tensor_copy(mixed[:], mixed_ps[:])
+                nc.sync.dma_start(out[:, t * P : (t + 1) * P], mixed[:])

@@ -24,9 +24,6 @@ def tile_deepseekv4mlaattention_kernel(tc, table, w, sink, offs, out):
         tc.tile_pool(name="held", bufs=1) as held,
         tc.psum_pool(name="psum", bufs=1) as psum,
     ):
-        offsets = held.tile([P, TOKENS * PIECE_COLS], U16, name="offsets")
-        nc.sync.dma_start(offsets[:], offs)
-
         rows = held.tile([P, BLOCKS, P], BF16, name="rows")
         table_blocks = table.rearrange("(b p) d -> p b d", p=P)
         for first in range(0, BLOCKS, CHUNK):
@@ -35,11 +32,14 @@ def tile_deepseekv4mlaattention_kernel(tc, table, w, sink, offs, out):
                 rows[:, first : first + CHUNK, :], table_blocks[:, first : first + CHUNK, :]
             )
 
+        offsets = held.tile([P, TOKENS * PIECE_COLS], U16, name="offsets")
+        nc.sync.dma_start(offsets[:], offs)
+
         queries = held.tile([P, TOKENS * P], BF16, name="queries")
-        nc.gpsimd.dma_start(queries[:], w)
+        nc.scalar.dma_start(queries[:], w)
 
         sink_row = held.tile([1, P], F32, name="sink_row")
-        nc.gpsimd.dma_start(sink_row[:], sink.rearrange("h one -> one h"))
+        nc.sync.dma_start(sink_row[:], sink.rearrange("h one -> one h"))
 
         identity = held.tile([P, P], BF16, name="identity")
         make_identity(nc, identity[:])

@@ -11,6 +11,7 @@ TOKENS = 2
 SLOTS = 2048
 BLOCKS = SLOTS // P
 CHUNK = 4
+CHUNKS = BLOCKS // CHUNK
 PIECE = 128
 PIECE_COLS = PIECE // 16
 SCALE = 192.0**-0.5
@@ -24,13 +25,11 @@ def tile_deepseekv4mlaattention_kernel(tc, table, w, sink, offs, out):
         tc.tile_pool(name="held", bufs=1) as held,
         tc.psum_pool(name="psum", bufs=1) as psum,
     ):
-        rows = held.tile([P, BLOCKS, P], BF16, name="rows")
-        table_blocks = table.rearrange("(b p) d -> p b d", p=P)
-        for first in range(0, BLOCKS, CHUNK):
-            queue = nc.sync if (first // CHUNK) % 2 == 0 else nc.scalar
-            queue.dma_start(
-                rows[:, first : first + CHUNK, :], table_blocks[:, first : first + CHUNK, :]
-            )
+        rows = held.tile([P, CHUNKS, CHUNK, P], BF16, name="rows")
+        table_chunks = table.rearrange("(c p k) d -> c p k d", p=P, k=CHUNK)
+        for c in range(CHUNKS):
+            queue = nc.sync if c % 2 == 0 else nc.scalar
+            queue.dma_start(rows[:, c, :, :], table_chunks[c])
 
         offsets = held.tile([P, TOKENS * PIECE_COLS], U16, name="offsets")
         nc.sync.dma_start(offsets[:], offs)
@@ -54,17 +53,18 @@ def tile_deepseekv4mlaattention_kernel(tc, table, w, sink, offs, out):
 
         flipped = held.tile([P, SLOTS], BF16, name="flipped")
         with tc.psum_pool(name="flip_psum", bufs=1) as flip_psum:
-            for first in range(0, BLOCKS, CHUNK):
-                flipped_ps = flip_psum.tile([P, CHUNK * P], BF16, name=f"flipped_ps{first}")
+            for c in range(CHUNKS):
+                flipped_ps = flip_psum.tile([P, CHUNK, P], BF16, name=f"flipped_ps{c}")
                 for k in range(CHUNK):
-                    nc.tensor.transpose(
-                        flipped_ps[:, k * P : (k + 1) * P], rows[:, first + k, :], identity[:]
-                    )
-                chunk_of_window = flipped[:, first * P : (first + CHUNK) * P]
-                if (first // CHUNK) % 2 == 0:
-                    nc.vector.tensor_copy(chunk_of_window, flipped_ps[:])
+                    nc.tensor.transpose(flipped_ps[:, k, :], rows[:, c, k, :], identity[:])
+                in_slot_order = flipped_ps[:].rearrange("d k p -> d p k")
+                chunk_of_window = flipped[:, c * CHUNK * P : (c + 1) * CHUNK * P].rearrange(
+                    "d (p k) -> d p k", k=CHUNK
+                )
+                if c % 2 == 0:
+                    nc.vector.tensor_copy(chunk_of_window, in_slot_order)
                 else:
-                    nc.scalar.copy(chunk_of_window, flipped_ps[:])
+                    nc.scalar.copy(chunk_of_window, in_slot_order)
 
         logits = [psum.tile([P, PIECE + 1], F32, name=f"logits{t}") for t in range(TOKENS)]
         for t in range(TOKENS):

@@ -3,8 +3,7 @@ from concourse.masks import make_identity
 
 BF16, F32, U16 = mybir.dt.bfloat16, mybir.dt.float32, mybir.dt.uint16
 EXP = mybir.ActivationFunctionType.Exp
-MULT = mybir.AluOpType.mult
-FREE_AXIS = mybir.AxisListType.X
+MULT, MIN = mybir.AluOpType.mult, mybir.AluOpType.min
 
 P = 128
 TOKENS = 2
@@ -51,6 +50,12 @@ def tile_deepseekv4mlaattention_kernel(tc, table, w, sink, offs, out):
         nc.vector.memset(zero[:], 0.0)
         nc.scalar.activation(one[:], zero[:], EXP)
 
+        logits = [psum.tile([P, PIECE + 1], F32, name=f"logits{t}") for t in range(TOKENS)]
+        for t in range(TOKENS):
+            nc.tensor.matmul(
+                logits[t][:, PIECE : PIECE + 1], sink_row[:], unscale[:], start=True, stop=True
+            )
+
         flipped = held.tile([P, SLOTS], BF16, name="flipped")
         with tc.psum_pool(name="flip_psum", bufs=1) as flip_psum:
             for c in range(CHUNKS):
@@ -66,11 +71,6 @@ def tile_deepseekv4mlaattention_kernel(tc, table, w, sink, offs, out):
                 else:
                     nc.scalar.copy(chunk_of_window, in_slot_order)
 
-        logits = [psum.tile([P, PIECE + 1], F32, name=f"logits{t}") for t in range(TOKENS)]
-        for t in range(TOKENS):
-            nc.tensor.matmul(
-                logits[t][:, PIECE : PIECE + 1], sink_row[:], unscale[:], start=True, stop=True
-            )
         for t in range(TOKENS):
             piece = offsets[:, t * PIECE_COLS : (t + 1) * PIECE_COLS]
             nc.tensor.matmul(
@@ -85,42 +85,54 @@ def tile_deepseekv4mlaattention_kernel(tc, table, w, sink, offs, out):
         nc.tensor.matmul(
             picked_ps[:], identity[:], flipped[:].indirect(offsets[:]), start=True, stop=True
         )
-        picked = held.tile([P, TOKENS * PIECE], BF16, name="picked")
-        nc.vector.tensor_copy(picked[:], picked_ps[:])
-        values_ps = psum.tile([P, TOKENS * P], BF16, name="values_ps")
-        for t in range(TOKENS):
-            nc.tensor.transpose(
-                values_ps[:, t * P : (t + 1) * P], picked[:, t * PIECE : (t + 1) * PIECE], identity[:]
-            )
-        values = held.tile([P, TOKENS * P], BF16, name="values")
-        nc.scalar.copy(values[:], values_ps[:])
 
         with tc.psum_pool(name="late_psum", bufs=1) as late_psum:
+            weights = [held.tile([P, PIECE + 1], F32, name=f"weights{t}") for t in range(TOKENS)]
+            total = [held.tile([P, 1], F32, name=f"total{t}") for t in range(TOKENS)]
             for t in range(TOKENS):
-                top = held.tile([P, 1], F32, name=f"top{t}")
-                nc.vector.reduce_max(top[:], logits[t][:], axis=FREE_AXIS)
+                negated = held.tile([P, PIECE + 1], F32, name=f"negated{t}")
                 shift = held.tile([P, 1], F32, name=f"shift{t}")
-                nc.vector.tensor_scalar(shift[:], top[:], -SCALE, None, op0=MULT)
-
-                weights = held.tile([P, PIECE + 1], F32, name=f"weights{t}")
-                total = held.tile([P, 1], F32, name=f"total{t}")
-                nc.scalar.activation(
-                    weights[:], logits[t][:], EXP, bias=shift[:], scale=SCALE, accum_out=total[:]
+                nc.vector.tensor_scalar(
+                    negated[:], logits[t][:], -SCALE, None, op0=MULT, op1=MIN, accum_out=shift[:]
                 )
+                nc.scalar.activation(
+                    weights[t][:], negated[:], EXP, bias=shift[:], scale=-1.0, accum_out=total[t][:]
+                )
+
+            picked = held.tile([P, TOKENS * PIECE], BF16, name="picked")
+            nc.vector.tensor_copy(picked[:], picked_ps[:])
+            values_ps = psum.tile([P, TOKENS * P], BF16, name="values_ps")
+            for t in range(TOKENS):
+                nc.tensor.transpose(
+                    values_ps[:, t * P : (t + 1) * P],
+                    picked[:, t * PIECE : (t + 1) * PIECE],
+                    identity[:],
+                )
+            values = held.tile([P, TOKENS * P], BF16, name="values")
+            nc.scalar.copy(values[:], values_ps[:])
+
+            for t in range(TOKENS):
                 inverse = held.tile([P, 1], F32, name=f"inverse{t}")
-                nc.vector.reciprocal(inverse[:], total[:])
+                nc.vector.reciprocal(inverse[:], total[t][:])
                 probs = held.tile([P, PIECE], BF16, name=f"probs{t}")
-                nc.vector.tensor_scalar(probs[:], weights[:, 0:PIECE], inverse[:], None, op0=MULT)
+                nc.vector.tensor_scalar(probs[:], weights[t][:, 0:PIECE], inverse[:], None, op0=MULT)
 
                 probs_t_ps = late_psum.tile([P, P], BF16, name=f"probs_t_ps{t}")
                 nc.tensor.transpose(probs_t_ps[:], probs[:], identity[:])
                 probs_t = held.tile([P, P], BF16, name=f"probs_t{t}")
-                nc.vector.tensor_copy(probs_t[:], probs_t_ps[:])
+                if t == 0:
+                    nc.vector.tensor_copy(probs_t[:], probs_t_ps[:])
+                else:
+                    nc.scalar.copy(probs_t[:], probs_t_ps[:])
 
                 mixed_ps = late_psum.tile([P, P], F32, name=f"mixed_ps{t}")
                 nc.tensor.matmul(
                     mixed_ps[:], values[:, t * P : (t + 1) * P], probs_t[:], start=True, stop=True
                 )
                 mixed = held.tile([P, P], F32, name=f"mixed{t}")
-                nc.vector.tensor_copy(mixed[:], mixed_ps[:])
-                nc.sync.dma_start(out[:, t * P : (t + 1) * P], mixed[:])
+                if t == 0:
+                    nc.vector.tensor_copy(mixed[:], mixed_ps[:])
+                    nc.sync.dma_start(out[:, 0:P], mixed[:])
+                else:
+                    nc.scalar.copy(mixed[:], mixed_ps[:])
+                    nc.scalar.dma_start(out[:, P : 2 * P], mixed[:])

@@ -14,6 +14,8 @@ CHUNKS = BLOCKS // CHUNK
 PIECE = 128
 PIECE_COLS = PIECE // 16
 SCALE = 192.0**-0.5
+BANK = 512
+WARM_UP = 6
 
 FLOPS = 2 * (2 * TOKENS * P * PIECE * P)
 
@@ -49,6 +51,13 @@ def tile_deepseekv4mlaattention_kernel(tc, table, w, sink, offs, out):
         one = held.tile([P, 1], F32, name="one")
         nc.vector.memset(zero[:], 0.0)
         nc.scalar.activation(one[:], zero[:], EXP)
+
+        zeros = held.tile([P, BANK], BF16, name="zeros")
+        nc.vector.memset(zeros[:], 0.0)
+        with tc.psum_pool(name="warm_psum", bufs=1) as warm_psum:
+            unread = warm_psum.tile([P, BANK], F32, name="unread")
+            for repeat in range(WARM_UP):
+                nc.tensor.matmul(unread[:], zeros[:, 0:P], zeros[:], start=True, stop=True)
 
         logits = [psum.tile([P, PIECE + 1], F32, name=f"logits{t}") for t in range(TOKENS)]
         for t in range(TOKENS):

@@ -8,9 +8,8 @@ MULT, MIN = mybir.AluOpType.mult, mybir.AluOpType.min
 P = 128
 TOKENS = 2
 SLOTS = 2048
-BLOCKS = SLOTS // P
 CHUNK = 4
-CHUNKS = BLOCKS // CHUNK
+CHUNKS = SLOTS // (CHUNK * P)
 PIECE = 128
 PIECE_COLS = PIECE // 16
 SCALE = 192.0**-0.5
@@ -22,10 +21,14 @@ FLOPS = 2 * (2 * TOKENS * P * PIECE * P)
 
 def tile_deepseekv4mlaattention_kernel(tc, table, w, sink, offs, out):
     nc = tc.nc
-    with (
-        tc.tile_pool(name="held", bufs=1) as held,
-        tc.psum_pool(name="psum", bufs=1) as psum,
-    ):
+
+    def copy_from_psum(turn, sbuf_side, psum_side):
+        if turn % 2 == 0:
+            nc.vector.tensor_copy(sbuf_side, psum_side)
+        else:
+            nc.scalar.copy(sbuf_side, psum_side)
+
+    with tc.tile_pool(name="held", bufs=1) as held:
         rows = held.tile([P, CHUNKS, CHUNK, P], BF16, name="rows")
         table_chunks = table.rearrange("(c p k) d -> c p k d", p=P, k=CHUNK)
         for c in range(CHUNKS):
@@ -43,6 +46,8 @@ def tile_deepseekv4mlaattention_kernel(tc, table, w, sink, offs, out):
 
         identity = held.tile([P, P], BF16, name="identity")
         make_identity(nc, identity[:])
+        identity_f32 = held.tile([P, P], F32, name="identity_f32")
+        make_identity(nc, identity_f32[:])
 
         unscale = held.tile([1, 1], F32, name="unscale")
         nc.vector.memset(unscale[:], 1.0 / SCALE)
@@ -59,45 +64,45 @@ def tile_deepseekv4mlaattention_kernel(tc, table, w, sink, offs, out):
             for repeat in range(WARM_UP):
                 nc.tensor.matmul(unread[:], zeros[:, 0:P], zeros[:], start=True, stop=True)
 
-        logits = [psum.tile([P, PIECE + 1], F32, name=f"logits{t}") for t in range(TOKENS)]
-        for t in range(TOKENS):
-            nc.tensor.matmul(
-                logits[t][:, PIECE : PIECE + 1], sink_row[:], unscale[:], start=True, stop=True
-            )
+        weights = [held.tile([P, PIECE + 1], BF16, name=f"weights{t}") for t in range(TOKENS)]
+        total = [held.tile([P, 1], F32, name=f"total{t}") for t in range(TOKENS)]
+        picked = held.tile([P, TOKENS * PIECE], BF16, name="picked")
 
-        flipped = held.tile([P, SLOTS], BF16, name="flipped")
-        with tc.psum_pool(name="flip_psum", bufs=1) as flip_psum:
-            for c in range(CHUNKS):
-                flipped_ps = flip_psum.tile([P, CHUNK, P], BF16, name=f"flipped_ps{c}")
-                for k in range(CHUNK):
-                    nc.tensor.transpose(flipped_ps[:, k, :], rows[:, c, k, :], identity[:])
-                in_slot_order = flipped_ps[:].rearrange("d k p -> d p k")
-                chunk_of_window = flipped[:, c * CHUNK * P : (c + 1) * CHUNK * P].rearrange(
-                    "d (p k) -> d p k", k=CHUNK
+        with tc.psum_pool(name="score_psum", bufs=1) as score_psum:
+            logits = [score_psum.tile([P, PIECE + 1], F32, name=f"logits{t}") for t in range(TOKENS)]
+            for t in range(TOKENS):
+                nc.tensor.matmul(
+                    logits[t][:, PIECE : PIECE + 1], sink_row[:], unscale[:], start=True, stop=True
                 )
-                if c % 2 == 0:
-                    nc.vector.tensor_copy(chunk_of_window, in_slot_order)
-                else:
-                    nc.scalar.copy(chunk_of_window, in_slot_order)
 
-        for t in range(TOKENS):
-            piece = offsets[:, t * PIECE_COLS : (t + 1) * PIECE_COLS]
+            flipped = held.tile([P, SLOTS], BF16, name="flipped")
+            with tc.psum_pool(name="flip_psum", bufs=1) as flip_psum:
+                for c in range(CHUNKS):
+                    flipped_ps = flip_psum.tile([P, CHUNK, P], BF16, name=f"flipped_ps{c}")
+                    for k in range(CHUNK):
+                        nc.tensor.transpose(flipped_ps[:, k, :], rows[:, c, k, :], identity[:])
+                    chunk_of_window = flipped[:, c * CHUNK * P : (c + 1) * CHUNK * P]
+                    copy_from_psum(
+                        c,
+                        chunk_of_window.rearrange("d (p k) -> d p k", k=CHUNK),
+                        flipped_ps[:].rearrange("d k p -> d p k"),
+                    )
+
+            for t in range(TOKENS):
+                piece = offsets[:, t * PIECE_COLS : (t + 1) * PIECE_COLS]
+                nc.tensor.matmul(
+                    logits[t][:, 0:PIECE],
+                    queries[:, t * P : (t + 1) * P],
+                    flipped[:].indirect(piece),
+                    start=True,
+                    stop=True,
+                )
+
+            picked_ps = score_psum.tile([P, TOKENS * PIECE], F32, name="picked_ps")
             nc.tensor.matmul(
-                logits[t][:, 0:PIECE],
-                queries[:, t * P : (t + 1) * P],
-                flipped[:].indirect(piece),
-                start=True,
-                stop=True,
+                picked_ps[:], identity[:], flipped[:].indirect(offsets[:]), start=True, stop=True
             )
 
-        picked_ps = psum.tile([P, TOKENS * PIECE], F32, name="picked_ps")
-        nc.tensor.matmul(
-            picked_ps[:], identity[:], flipped[:].indirect(offsets[:]), start=True, stop=True
-        )
-
-        with tc.psum_pool(name="late_psum", bufs=1) as late_psum:
-            weights = [held.tile([P, PIECE + 1], F32, name=f"weights{t}") for t in range(TOKENS)]
-            total = [held.tile([P, 1], F32, name=f"total{t}") for t in range(TOKENS)]
             for t in range(TOKENS):
                 negated = held.tile([P, PIECE + 1], F32, name=f"negated{t}")
                 shift = held.tile([P, 1], F32, name=f"shift{t}")
@@ -108,9 +113,10 @@ def tile_deepseekv4mlaattention_kernel(tc, table, w, sink, offs, out):
                     weights[t][:], negated[:], EXP, bias=shift[:], scale=-1.0, accum_out=total[t][:]
                 )
 
-            picked = held.tile([P, TOKENS * PIECE], BF16, name="picked")
             nc.vector.tensor_copy(picked[:], picked_ps[:])
-            values_ps = psum.tile([P, TOKENS * P], BF16, name="values_ps")
+
+        with tc.psum_pool(name="late_psum", bufs=1) as late_psum:
+            values_ps = late_psum.tile([P, TOKENS * P], BF16, name="values_ps")
             for t in range(TOKENS):
                 nc.tensor.transpose(
                     values_ps[:, t * P : (t + 1) * P],
@@ -120,28 +126,28 @@ def tile_deepseekv4mlaattention_kernel(tc, table, w, sink, offs, out):
             values = held.tile([P, TOKENS * P], BF16, name="values")
             nc.scalar.copy(values[:], values_ps[:])
 
+            inverse = [held.tile([P, 1], F32, name=f"inverse{t}") for t in range(TOKENS)]
             for t in range(TOKENS):
-                inverse = held.tile([P, 1], F32, name=f"inverse{t}")
-                nc.vector.reciprocal(inverse[:], total[t][:])
-                probs = held.tile([P, PIECE], BF16, name=f"probs{t}")
-                nc.vector.tensor_scalar(probs[:], weights[t][:, 0:PIECE], inverse[:], None, op0=MULT)
+                nc.vector.reciprocal(inverse[t][:], total[t][:])
 
-                probs_t_ps = late_psum.tile([P, P], BF16, name=f"probs_t_ps{t}")
-                nc.tensor.transpose(probs_t_ps[:], probs[:], identity[:])
-                probs_t = held.tile([P, P], BF16, name=f"probs_t{t}")
-                if t == 0:
-                    nc.vector.tensor_copy(probs_t[:], probs_t_ps[:])
-                else:
-                    nc.scalar.copy(probs_t[:], probs_t_ps[:])
+            weights_t = [held.tile([P, P], BF16, name=f"weights_t{t}") for t in range(TOKENS)]
+            for t in range(TOKENS):
+                weights_t_ps = late_psum.tile([P, P], BF16, name=f"weights_t_ps{t}")
+                nc.tensor.transpose(weights_t_ps[:], weights[t][:, 0:PIECE], identity[:])
+                copy_from_psum(t, weights_t[t][:], weights_t_ps[:])
 
+            spread = [held.tile([P, P], F32, name=f"spread{t}") for t in range(TOKENS)]
+            for t in range(TOKENS):
+                spread_ps = late_psum.tile([P, P], F32, name=f"spread_ps{t}")
+                nc.tensor.transpose(spread_ps[:], inverse[t][:].to_broadcast([P, P]), identity_f32[:])
+                copy_from_psum(t, spread[t][:], spread_ps[:])
+
+            for t in range(TOKENS):
                 mixed_ps = late_psum.tile([P, P], F32, name=f"mixed_ps{t}")
                 nc.tensor.matmul(
-                    mixed_ps[:], values[:, t * P : (t + 1) * P], probs_t[:], start=True, stop=True
+                    mixed_ps[:], values[:, t * P : (t + 1) * P], weights_t[t][:], start=True, stop=True
                 )
                 mixed = held.tile([P, P], F32, name=f"mixed{t}")
-                if t == 0:
-                    nc.vector.tensor_copy(mixed[:], mixed_ps[:])
-                    nc.sync.dma_start(out[:, 0:P], mixed[:])
-                else:
-                    nc.scalar.copy(mixed[:], mixed_ps[:])
-                    nc.scalar.dma_start(out[:, P : 2 * P], mixed[:])
+                nc.vector.tensor_tensor(mixed[:], mixed_ps[:], spread[t][:], MULT)
+                queue = nc.sync if t == 0 else nc.scalar
+                queue.dma_start(out[:, t * P : (t + 1) * P], mixed[:])

@@ -8,8 +8,9 @@ MULT, MIN = mybir.AluOpType.mult, mybir.AluOpType.min
 P = 128
 TOKENS = 2
 SLOTS = 2048
+BLOCKS = SLOTS // P
 CHUNK = 4
-CHUNKS = SLOTS // (CHUNK * P)
+CHUNKS = BLOCKS // CHUNK
 PIECE = 128
 PIECE_COLS = PIECE // 16
 SCALE = 192.0**-0.5
@@ -21,14 +22,10 @@ FLOPS = 2 * (2 * TOKENS * P * PIECE * P)
 
 def tile_deepseekv4mlaattention_kernel(tc, table, w, sink, offs, out):
     nc = tc.nc
-
-    def copy_from_psum(turn, sbuf_side, psum_side):
-        if turn % 2 == 0:
-            nc.vector.tensor_copy(sbuf_side, psum_side)
-        else:
-            nc.scalar.copy(sbuf_side, psum_side)
-
-    with tc.tile_pool(name="held", bufs=1) as held:
+    with (
+        tc.tile_pool(name="held", bufs=1) as held,
+        tc.psum_pool(name="psum", bufs=1) as psum,
+    ):
         rows = held.tile([P, CHUNKS, CHUNK, P], BF16, name="rows")
         table_chunks = table.rearrange("(c p k) d -> c p k d", p=P, k=CHUNK)
         for c in range(CHUNKS):
@@ -46,8 +43,6 @@ def tile_deepseekv4mlaattention_kernel(tc, table, w, sink, offs, out):
 
         identity = held.tile([P, P], BF16, name="identity")
         make_identity(nc, identity[:])
-        identity_f32 = held.tile([P, P], F32, name="identity_f32")
-        make_identity(nc, identity_f32[:])
 
         unscale = held.tile([1, 1], F32, name="unscale")
         nc.vector.memset(unscale[:], 1.0 / SCALE)
@@ -64,45 +59,44 @@ def tile_deepseekv4mlaattention_kernel(tc, table, w, sink, offs, out):
             for repeat in range(WARM_UP):
                 nc.tensor.matmul(unread[:], zeros[:, 0:P], zeros[:], start=True, stop=True)
 
-        weights = [held.tile([P, PIECE + 1], BF16, name=f"weights{t}") for t in range(TOKENS)]
-        total = [held.tile([P, 1], F32, name=f"total{t}") for t in range(TOKENS)]
-        picked = held.tile([P, TOKENS * PIECE], BF16, name="picked")
-
-        with tc.psum_pool(name="score_psum", bufs=1) as score_psum:
-            logits = [score_psum.tile([P, PIECE + 1], F32, name=f"logits{t}") for t in range(TOKENS)]
-            for t in range(TOKENS):
-                nc.tensor.matmul(
-                    logits[t][:, PIECE : PIECE + 1], sink_row[:], unscale[:], start=True, stop=True
+        flipped = held.tile([P, SLOTS], BF16, name="flipped")
+        with tc.psum_pool(name="flip_psum", bufs=1) as flip_psum:
+            for c in range(CHUNKS):
+                flipped_ps = flip_psum.tile([P, CHUNK, P], BF16, name=f"flipped_ps{c}")
+                for k in range(CHUNK):
+                    nc.tensor.transpose(flipped_ps[:, k, :], rows[:, c, k, :], identity[:])
+                in_slot_order = flipped_ps[:].rearrange("d k p -> d p k")
+                chunk_of_window = flipped[:, c * CHUNK * P : (c + 1) * CHUNK * P].rearrange(
+                    "d (p k) -> d p k", k=CHUNK
                 )
+                if c % 2 == 0:
+                    nc.vector.tensor_copy(chunk_of_window, in_slot_order)
+                else:
+                    nc.scalar.copy(chunk_of_window, in_slot_order)
 
-            flipped = held.tile([P, SLOTS], BF16, name="flipped")
-            with tc.psum_pool(name="flip_psum", bufs=1) as flip_psum:
-                for c in range(CHUNKS):
-                    flipped_ps = flip_psum.tile([P, CHUNK, P], BF16, name=f"flipped_ps{c}")
-                    for k in range(CHUNK):
-                        nc.tensor.transpose(flipped_ps[:, k, :], rows[:, c, k, :], identity[:])
-                    chunk_of_window = flipped[:, c * CHUNK * P : (c + 1) * CHUNK * P]
-                    copy_from_psum(
-                        c,
-                        chunk_of_window.rearrange("d (p k) -> d p k", k=CHUNK),
-                        flipped_ps[:].rearrange("d k p -> d p k"),
-                    )
-
-            for t in range(TOKENS):
-                piece = offsets[:, t * PIECE_COLS : (t + 1) * PIECE_COLS]
-                nc.tensor.matmul(
-                    logits[t][:, 0:PIECE],
-                    queries[:, t * P : (t + 1) * P],
-                    flipped[:].indirect(piece),
-                    start=True,
-                    stop=True,
-                )
-
-            picked_ps = score_psum.tile([P, TOKENS * PIECE], F32, name="picked_ps")
+        logits = [psum.tile([P, PIECE + 1], F32, name=f"logits{t}") for t in range(TOKENS)]
+        for t in range(TOKENS):
             nc.tensor.matmul(
-                picked_ps[:], identity[:], flipped[:].indirect(offsets[:]), start=True, stop=True
+                logits[t][:, PIECE : PIECE + 1], sink_row[:], unscale[:], start=True, stop=True
+            )
+        for t in range(TOKENS):
+            piece = offsets[:, t * PIECE_COLS : (t + 1) * PIECE_COLS]
+            nc.tensor.matmul(
+                logits[t][:, 0:PIECE],
+                queries[:, t * P : (t + 1) * P],
+                flipped[:].indirect(piece),
+                start=True,
+                stop=True,
             )
 
+        picked_ps = psum.tile([P, TOKENS * PIECE], F32, name="picked_ps")
+        nc.tensor.matmul(
+            picked_ps[:], identity[:], flipped[:].indirect(offsets[:]), start=True, stop=True
+        )
+
+        with tc.psum_pool(name="late_psum", bufs=1) as late_psum:
+            weights = [held.tile([P, PIECE + 1], F32, name=f"weights{t}") for t in range(TOKENS)]
+            total = [held.tile([P, 1], F32, name=f"total{t}") for t in range(TOKENS)]
             for t in range(TOKENS):
                 negated = held.tile([P, PIECE + 1], F32, name=f"negated{t}")
                 shift = held.tile([P, 1], F32, name=f"shift{t}")
@@ -113,10 +107,9 @@ def tile_deepseekv4mlaattention_kernel(tc, table, w, sink, offs, out):
                     weights[t][:], negated[:], EXP, bias=shift[:], scale=-1.0, accum_out=total[t][:]
                 )
 
+            picked = held.tile([P, TOKENS * PIECE], BF16, name="picked")
             nc.vector.tensor_copy(picked[:], picked_ps[:])
-
-        with tc.psum_pool(name="late_psum", bufs=1) as late_psum:
-            values_ps = late_psum.tile([P, TOKENS * P], BF16, name="values_ps")
+            values_ps = psum.tile([P, TOKENS * P], BF16, name="values_ps")
             for t in range(TOKENS):
                 nc.tensor.transpose(
                     values_ps[:, t * P : (t + 1) * P],
@@ -126,28 +119,28 @@ def tile_deepseekv4mlaattention_kernel(tc, table, w, sink, offs, out):
             values = held.tile([P, TOKENS * P], BF16, name="values")
             nc.scalar.copy(values[:], values_ps[:])
 
-            inverse = [held.tile([P, 1], F32, name=f"inverse{t}") for t in range(TOKENS)]
             for t in range(TOKENS):
-                nc.vector.reciprocal(inverse[t][:], total[t][:])
+                inverse = held.tile([P, 1], F32, name=f"inverse{t}")
+                nc.vector.reciprocal(inverse[:], total[t][:])
+                probs = held.tile([P, PIECE], BF16, name=f"probs{t}")
+                nc.vector.tensor_scalar(probs[:], weights[t][:, 0:PIECE], inverse[:], None, op0=MULT)
 
-            weights_t = [held.tile([P, P], BF16, name=f"weights_t{t}") for t in range(TOKENS)]
-            for t in range(TOKENS):
-                weights_t_ps = late_psum.tile([P, P], BF16, name=f"weights_t_ps{t}")
-                nc.tensor.transpose(weights_t_ps[:], weights[t][:, 0:PIECE], identity[:])
-                copy_from_psum(t, weights_t[t][:], weights_t_ps[:])
+                probs_t_ps = late_psum.tile([P, P], BF16, name=f"probs_t_ps{t}")
+                nc.tensor.transpose(probs_t_ps[:], probs[:], identity[:])
+                probs_t = held.tile([P, P], BF16, name=f"probs_t{t}")
+                if t == 0:
+                    nc.vector.tensor_copy(probs_t[:], probs_t_ps[:])
+                else:
+                    nc.scalar.copy(probs_t[:], probs_t_ps[:])
 
-            spread = [held.tile([P, P], F32, name=f"spread{t}") for t in range(TOKENS)]
-            for t in range(TOKENS):
-                spread_ps = late_psum.tile([P, P], F32, name=f"spread_ps{t}")
-                nc.tensor.transpose(spread_ps[:], inverse[t][:].to_broadcast([P, P]), identity_f32[:])
-                copy_from_psum(t, spread[t][:], spread_ps[:])
-
-            for t in range(TOKENS):
                 mixed_ps = late_psum.tile([P, P], F32, name=f"mixed_ps{t}")
                 nc.tensor.matmul(
-                    mixed_ps[:], values[:, t * P : (t + 1) * P], weights_t[t][:], start=True, stop=True
+                    mixed_ps[:], values[:, t * P : (t + 1) * P], probs_t[:], start=True, stop=True
                 )
                 mixed = held.tile([P, P], F32, name=f"mixed{t}")
-                nc.vector.tensor_tensor(mixed[:], mixed_ps[:], spread[t][:], MULT)
-                queue = nc.sync if t == 0 else nc.scalar
-                queue.dma_start(out[:, t * P : (t + 1) * P], mixed[:])
+                if t == 0:
+                    nc.vector.tensor_copy(mixed[:], mixed_ps[:])
+                    nc.sync.dma_start(out[:, 0:P], mixed[:])
+                else:
+                    nc.scalar.copy(mixed[:], mixed_ps[:])
+                    nc.scalar.dma_start(out[:, P : 2 * P], mixed[:])

import concourse.mybir as mybir
from concourse.masks import make_identity

BF16, F32, U16 = mybir.dt.bfloat16, mybir.dt.float32, mybir.dt.uint16
EXP = mybir.ActivationFunctionType.Exp
MULT, MIN = mybir.AluOpType.mult, mybir.AluOpType.min

P = 128
TOKENS = 2
SLOTS = 2048
BLOCKS = SLOTS // P
CHUNK = 4
CHUNKS = BLOCKS // CHUNK
PIECE = 128
PIECE_COLS = PIECE // 16
SCALE = 192.0**-0.5
BANK = 512
WARM_UP = 6

FLOPS = 2 * (2 * TOKENS * P * PIECE * P)


def tile_deepseekv4mlaattention_kernel(tc, table, w, sink, offs, out):
    nc = tc.nc
    with (
        tc.tile_pool(name="held", bufs=1) as held,
        tc.psum_pool(name="psum", bufs=1) as psum,
    ):
        rows = held.tile([P, CHUNKS, CHUNK, P], BF16, name="rows")
        table_chunks = table.rearrange("(c p k) d -> c p k d", p=P, k=CHUNK)
        for c in range(CHUNKS):
            queue = nc.sync if c % 2 == 0 else nc.scalar
            queue.dma_start(rows[:, c, :, :], table_chunks[c])

        offsets = held.tile([P, TOKENS * PIECE_COLS], U16, name="offsets")
        nc.sync.dma_start(offsets[:], offs)

        queries = held.tile([P, TOKENS * P], BF16, name="queries")
        nc.scalar.dma_start(queries[:], w)

        sink_row = held.tile([1, P], F32, name="sink_row")
        nc.sync.dma_start(sink_row[:], sink.rearrange("h one -> one h"))

        identity = held.tile([P, P], BF16, name="identity")
        make_identity(nc, identity[:])

        unscale = held.tile([1, 1], F32, name="unscale")
        nc.vector.memset(unscale[:], 1.0 / SCALE)

        zero = held.tile([P, 1], F32, name="zero")
        one = held.tile([P, 1], F32, name="one")
        nc.vector.memset(zero[:], 0.0)
        nc.scalar.activation(one[:], zero[:], EXP)

        zeros = held.tile([P, BANK], BF16, name="zeros")
        nc.vector.memset(zeros[:], 0.0)
        with tc.psum_pool(name="warm_psum", bufs=1) as warm_psum:
            unread = warm_psum.tile([P, BANK], F32, name="unread")
            for repeat in range(WARM_UP):
                nc.tensor.matmul(unread[:], zeros[:, 0:P], zeros[:], start=True, stop=True)

        flipped = held.tile([P, SLOTS], BF16, name="flipped")
        with tc.psum_pool(name="flip_psum", bufs=1) as flip_psum:
            for c in range(CHUNKS):
                flipped_ps = flip_psum.tile([P, CHUNK, P], BF16, name=f"flipped_ps{c}")
                for k in range(CHUNK):
                    nc.tensor.transpose(flipped_ps[:, k, :], rows[:, c, k, :], identity[:])
                in_slot_order = flipped_ps[:].rearrange("d k p -> d p k")
                chunk_of_window = flipped[:, c * CHUNK * P : (c + 1) * CHUNK * P].rearrange(
                    "d (p k) -> d p k", k=CHUNK
                )
                if c % 2 == 0:
                    nc.vector.tensor_copy(chunk_of_window, in_slot_order)
                else:
                    nc.scalar.copy(chunk_of_window, in_slot_order)

        logits = [psum.tile([P, PIECE + 1], F32, name=f"logits{t}") for t in range(TOKENS)]
        for t in range(TOKENS):
            nc.tensor.matmul(
                logits[t][:, PIECE : PIECE + 1], sink_row[:], unscale[:], start=True, stop=True
            )
        for t in range(TOKENS):
            piece = offsets[:, t * PIECE_COLS : (t + 1) * PIECE_COLS]
            nc.tensor.matmul(
                logits[t][:, 0:PIECE],
                queries[:, t * P : (t + 1) * P],
                flipped[:].indirect(piece),
                start=True,
                stop=True,
            )

        picked_ps = psum.tile([P, TOKENS * PIECE], F32, name="picked_ps")
        nc.tensor.matmul(
            picked_ps[:], identity[:], flipped[:].indirect(offsets[:]), start=True, stop=True
        )

        with tc.psum_pool(name="late_psum", bufs=1) as late_psum:
            weights = [held.tile([P, PIECE + 1], F32, name=f"weights{t}") for t in range(TOKENS)]
            total = [held.tile([P, 1], F32, name=f"total{t}") for t in range(TOKENS)]
            for t in range(TOKENS):
                negated = held.tile([P, PIECE + 1], F32, name=f"negated{t}")
                shift = held.tile([P, 1], F32, name=f"shift{t}")
                nc.vector.tensor_scalar(
                    negated[:], logits[t][:], -SCALE, None, op0=MULT, op1=MIN, accum_out=shift[:]
                )
                nc.scalar.activation(
                    weights[t][:], negated[:], EXP, bias=shift[:], scale=-1.0, accum_out=total[t][:]
                )

            picked = held.tile([P, TOKENS * PIECE], BF16, name="picked")
            nc.vector.tensor_copy(picked[:], picked_ps[:])
            values_ps = psum.tile([P, TOKENS * P], BF16, name="values_ps")
            for t in range(TOKENS):
                nc.tensor.transpose(
                    values_ps[:, t * P : (t + 1) * P],
                    picked[:, t * PIECE : (t + 1) * PIECE],
                    identity[:],
                )
            values = held.tile([P, TOKENS * P], BF16, name="values")
            nc.scalar.copy(values[:], values_ps[:])

            for t in range(TOKENS):
                inverse = held.tile([P, 1], F32, name=f"inverse{t}")
                nc.vector.reciprocal(inverse[:], total[t][:])
                probs = held.tile([P, PIECE], BF16, name=f"probs{t}")
                nc.vector.tensor_scalar(probs[:], weights[t][:, 0:PIECE], inverse[:], None, op0=MULT)

                probs_t_ps = late_psum.tile([P, P], BF16, name=f"probs_t_ps{t}")
                nc.tensor.transpose(probs_t_ps[:], probs[:], identity[:])
                probs_t = held.tile([P, P], BF16, name=f"probs_t{t}")
                if t == 0:
                    nc.vector.tensor_copy(probs_t[:], probs_t_ps[:])
                else:
                    nc.scalar.copy(probs_t[:], probs_t_ps[:])

                mixed_ps = late_psum.tile([P, P], F32, name=f"mixed_ps{t}")
                nc.tensor.matmul(
                    mixed_ps[:], values[:, t * P : (t + 1) * P], probs_t[:], start=True, stop=True
                )
                mixed = held.tile([P, P], F32, name=f"mixed{t}")
                if t == 0:
                    nc.vector.tensor_copy(mixed[:], mixed_ps[:])
                    nc.sync.dma_start(out[:, 0:P], mixed[:])
                else:
                    nc.scalar.copy(mixed[:], mixed_ps[:])
                    nc.scalar.dma_start(out[:, P : 2 * P], mixed[:])
